import numpy as np
import ml_dtypes


def mxq(x, axis, fmt="e4m3"):
    dtype, down = {"e4m3": (ml_dtypes.float8_e4m3fn, 7), "e5m2": (ml_dtypes.float8_e5m2, 14)}[fmt]
    v = np.moveaxis(np.asarray(x, np.float32).astype(ml_dtypes.bfloat16).astype(np.float64), axis, -1)
    blocks = v.reshape(v.shape[:-1] + (-1, 32))
    amax = np.abs(blocks).max(-1, keepdims=True)
    byte = np.maximum(np.where(amax > 0, np.frexp(amax)[1] - 1 + 127, 0) - down, 1)
    scale = np.exp2(byte - 127.0)
    codes = (blocks / scale).astype(np.float32).astype(dtype).astype(np.float64)
    return np.moveaxis((codes * scale).reshape(v.shape), -1, axis)


WIDE = False


def mx_kscale(k):
    if not WIDE:
        return np.ones(k)
    levels = np.array([10, -10, 5, -5, 0])
    a = np.random.permutation(np.resize(levels, k // 512 * 4)).reshape(k // 512, 4)
    idx = np.arange(k)
    return np.exp2(a[idx // 512, idx % 128 // 32])


BF16 = ml_dtypes.bfloat16


def bf(x):
    return np.asarray(x, np.float32).astype(BF16)


def f64(x):
    return np.asarray(x).astype(np.float64)


B, N, DIM, H, KD, D = 4, 256, 1024, 12, 64, 128
DH = H * D
EPS = 1e-5


def hard_swish(v):
    return v * (np.minimum(np.maximum(v + 3.0, 0.0), 6.0) / 6.0)


def setup_inputs():
    t = mx_kscale(DH)
    c = 2.0 ** (-8.0 * np.random.random(DIM))
    return {"h_attn": bf(1.5 * np.random.standard_normal((B, N, DH)) * t),
            "proj_w": bf(np.random.standard_normal((DIM, DH)) * c[:, None] / np.sqrt(DH) / t),
            "proj_g": bf(1.0 + 0.1 * np.random.standard_normal(DIM)),
            "proj_b": bf(0.1 * np.random.standard_normal(DIM))}


def bn(y, g, b):
    m = y.mean(axis=(0, 1))
    v = ((y - m) ** 2).mean(axis=(0, 1))
    return (y - m) * (g / np.sqrt(v + EPS)) + b


def reference(h_attn, proj_w, proj_g, proj_b):
    h = hard_swish(f64(h_attn))
    y = mxq(h, 2, "e4m3") @ mxq(f64(proj_w), 1, "e4m3").T
    return bn(y, f64(proj_g), f64(proj_b))

@@ -1,0 +1,225 @@
+import concourse.mybir as mybir
+from concourse.masks import make_identity
+
+F32 = mybir.dt.float32
+BF16 = mybir.dt.bfloat16
+U32 = mybir.dt.uint32
+U8 = mybir.dt.uint8
+FP8X4 = mybir.dt.float8_e4m3fn_x4
+ACT = mybir.ActivationFunctionType
+ALU = mybir.AluOpType
+
+P = 128
+ROWS = 1024
+FEATS = 1024
+K = 1536
+K_PASS = 512
+K_HALF = 256
+PASSES = K // K_PASS
+BANK = 512
+HALVES = 2
+FEAT_TILES = FEATS // P
+ROW_TILES = ROWS // P
+BLK = 64
+JOB = 256
+IN_FLIGHT = 3
+EPS = 1e-5
+
+FLOPS = 2 * ROWS * FEATS * K
+
+
+def tile_attention_pb_kernel(tc, h_attn, proj_w, proj_g, proj_b, out):
+    nc = tc.nc
+    h_flat = h_attn.flatten_outer_dims()
+    out_flat = out.flatten_outer_dims()
+
+    with tc.tile_pool(name="keep", bufs=1) as keep, tc.tile_pool(name="work", bufs=3) as work, tc.tile_pool(
+        name="small", bufs=4
+    ) as small, tc.psum_pool(name="psum", bufs=1) as psum, tc.manual_schedule():
+        gb_rows = keep.tile([P, P], BF16)
+        nc.vector.memset(gb_rows[:], 0.0)
+        nc.sync.dma_start(out=gb_rows[0:FEAT_TILES, :], in_=proj_g.rearrange("(f p) -> f p", p=P))
+        nc.sync.dma_start(out=gb_rows[FEAT_TILES : 2 * FEAT_TILES, :], in_=proj_b.rearrange("(f p) -> f p", p=P))
+
+        w_raw = {}
+        h_raw = {}
+        for g in range(PASSES):
+            for half in range(HALVES):
+                w_piece = keep.tile([P, BANK // P, K_PASS], BF16, name="w_raw_%d_%d" % (g, half))
+                nc.sync.dma_start(
+                    out=w_piece[:],
+                    in_=proj_w[half * BANK : (half + 1) * BANK, g * K_PASS : (g + 1) * K_PASS].rearrange(
+                        "(i p) k -> p i k", p=P
+                    ),
+                )
+                w_raw[(g, half)] = w_piece
+                h_piece = keep.tile([P, BANK // BLK, K_HALF], BF16, name="h_raw_%d_%d" % (g, half))
+                for u in range(2):
+                    k0 = g * K_PASS + u * K_HALF
+                    nc.sync.dma_start(
+                        out=h_piece[u:P:2, :, :],
+                        in_=h_flat[half * BANK : (half + 1) * BANK, k0 : k0 + K_HALF].rearrange(
+                            "(blk r) k -> r blk k", r=BLK
+                        ),
+                    )
+                h_raw[(g, half)] = h_piece
+
+        ident = keep.tile([P, P], F32)
+        make_identity(nc, ident[:])
+
+        one = small.tile([P, 1], F32, tag="one")
+        nc.vector.memset(one[:], 1.0)
+        one_root = small.tile([P, 1], F32, tag="one_root")
+        nc.scalar.activation(out=one_root[:], in_=one[:], func=ACT.Sqrt)
+
+        gb_f32 = keep.tile([P, P], F32)
+        nc.vector.tensor_copy(out=gb_f32[:], in_=gb_rows[:])
+        gb_bank = psum.tile([P, BANK], F32, tag="bank6")
+        nc.tensor.transpose(gb_bank[:, 0:P], gb_f32[:], ident[:])
+        gb = keep.tile([P, 2 * FEAT_TILES], F32)
+        nc.vector.tensor_copy(out=gb[:], in_=gb_bank[:, 0 : 2 * FEAT_TILES])
+
+        h_codes = keep.tile([P, PASSES, ROWS], U32, align_bytes=64)
+        h_scales = keep.tile([P, PASSES, ROWS], U8, align_bytes=64)
+        w_codes = keep.tile([P, PASSES, FEATS], U32, align_bytes=64)
+        w_scales = keep.tile([P, PASSES, FEATS], U8, align_bytes=64)
+
+        def quantise_w(g, half):
+            for j in range(BANK // JOB):
+                bank = psum.tile([P, 2, JOB], F32, tag="bank%d" % (6 + j))
+                for i in range(JOB // P):
+                    for u in range(2):
+                        nc.tensor.transpose(
+                            bank[:, u, i * P : (i + 1) * P],
+                            w_raw[(g, half)][:, j * (JOB // P) + i, u * K_HALF : (u + 1) * K_HALF].bitcast(F32),
+                            ident[:],
+                        )
+                w_grouped = work.tile([P, 4 * JOB], BF16, align_bytes=64, tag="w_grouped")
+                nc.scalar.copy(
+                    out=w_grouped[:].bitcast(F32).rearrange("p (c u) -> p c u", u=2),
+                    in_=bank[:].rearrange("p u c -> p c u"),
+                )
+                cols = slice(half * BANK + j * JOB, half * BANK + (j + 1) * JOB)
+                nc.vector.quantize_mx(
+                    out=w_codes[:, g, cols].bitcast(FP8X4), scales=w_scales[:, g, cols], in_=w_grouped[:]
+                )
+
+        def quantise_h(g, half):
+            h_grouped = []
+            for j in range(BANK // JOB):
+                bank = psum.tile([P, BANK], F32, tag="bank%d" % (4 + j))
+                for i in range(JOB // BLK):
+                    nc.tensor.transpose(
+                        bank[:, i * P : (i + 1) * P],
+                        h_raw[(g, half)][:, j * (JOB // BLK) + i, :].bitcast(F32),
+                        ident[:],
+                    )
+                v = bank[:].bitcast(BF16)
+                ramp = work.tile([P, 4 * JOB], F32, tag="ramp")
+                nc.scalar.activation(out=ramp[:], in_=v, func=ACT.Relu, bias=0.5, scale=1.0 / 6.0)
+                h_bf16 = work.tile([P, 4 * JOB], BF16, align_bytes=64, tag="h_grouped")
+                nc.vector.scalar_tensor_tensor(
+                    out=h_bf16[:], in0=ramp[:], scalar=1.0, in1=v, op0=ALU.min, op1=ALU.mult
+                )
+                h_grouped.append(h_bf16)
+            for j in range(BANK // JOB):
+                cols = slice(half * BANK + j * JOB, half * BANK + (j + 1) * JOB)
+                nc.vector.quantize_mx(
+                    out=h_codes[:, g, cols].bitcast(FP8X4), scales=h_scales[:, g, cols], in_=h_grouped[j][:]
+                )
+
+        y = {}
+
+        def products(f, passes):
+            feats = slice(f * P, (f + 1) * P)
+            for half in range(HALVES):
+                rows = slice(half * BANK, (half + 1) * BANK)
+                if passes[0] == 0:
+                    acc = psum.tile([P, BANK], F32, tag="bank%d" % (2 * (f % IN_FLIGHT) + half))
+                    y[(f, half)] = acc
+                for g in passes:
+                    nc.tensor.matmul_mx(
+                        out=y[(f, half)][:],
+                        lhsT=w_codes[:, g, feats].bitcast(FP8X4),
+                        lhsT_scale=w_scales[:, g, feats],
+                        rhs=h_codes[:, g, rows].bitcast(FP8X4),
+                        rhs_scale=h_scales[:, g, rows],
+                        start=(g == 0),
+                        stop=(g == PASSES - 1),
+                    )
+
+        for g in range(PASSES):
+            for half in range(HALVES):
+                quantise_w(g, half)
+                quantise_h(g, half)
+                if g > 0 and half == 0:
+                    products(0, [g - 1])
+                    products(1, [g - 1])
+
+        mean_var = {}
+        std = {}
+        z = {}
+
+        def statistics(f):
+            stats = small.tile([P, HALVES, 6], F32, tag="stats")
+            for half in range(HALVES):
+                nc.vector.bn_stats(out=stats[:, half, :], in_=y[(f, half)][:])
+            mv = small.tile([P, 2], F32, tag="mean_var")
+            nc.vector.bn_aggr(out=mv[:], in_=stats[:].rearrange("p a s -> p (a s)"))
+            root = small.tile([P, 1], F32, tag="std")
+            nc.scalar.activation(out=root[:], in_=mv[:, 1:2], func=ACT.Sqrt, bias=EPS, scale=1.0)
+            mean_var[f] = mv
+            std[f] = root
+
+        def norm(f):
+            rstd = small.tile([P, 1], F32, tag="rstd")
+            nc.vector.reciprocal(out=rstd[:], in_=std[f][:])
+            scale = small.tile([P, 1], F32, tag="scale")
+            nc.vector.tensor_mul(out=scale[:], in0=rstd[:], in1=gb[:, f : f + 1])
+            mean_scaled = small.tile([P, 1], F32, tag="mean_scaled")
+            nc.vector.tensor_mul(out=mean_scaled[:], in0=mean_var[f][:, 0:1], in1=scale[:])
+            shift = small.tile([P, 1], F32, tag="shift")
+            nc.vector.tensor_sub(out=shift[:], in0=gb[:, FEAT_TILES + f : FEAT_TILES + f + 1], in1=mean_scaled[:])
+            normed = work.tile([P, ROWS], F32, tag="z")
+            for half in range(HALVES):
+                nc.scalar.activation(
+                    out=normed[:, half * BANK : (half + 1) * BANK],
+                    in_=y[(f, half)][:],
+                    func=ACT.Identity,
+                    bias=shift[:],
+                    scale=scale[:],
+                )
+            z[f] = normed
+
+        zt = {}
+
+        def transposes_back(f):
+            for j in range(2):
+                bank = psum.tile([P, ROW_TILES // 2, P], F32, tag="bank%d" % (6 + j))
+                for i in range(ROW_TILES // 2):
+                    m = j * (ROW_TILES // 2) + i
+                    nc.tensor.transpose(bank[:, i, :], z[f][:, m * P : (m + 1) * P], ident[:])
+                zt[(f, j)] = bank
+
+        def store(f):
+            o = work.tile([P, ROW_TILES, P], F32, tag="o")
+            nc.vector.tensor_copy(out=o[:, 0 : ROW_TILES // 2, :], in_=zt[(f, 0)][:])
+            nc.scalar.copy(out=o[:, ROW_TILES // 2 : ROW_TILES, :], in_=zt[(f, 1)][:])
+            nc.sync.dma_start(out=out_flat[:, f * P : (f + 1) * P].rearrange("(m p) c -> p m c", p=P), in_=o[:])
+
+        products(0, [PASSES - 1])
+        products(1, [PASSES - 1])
+        products(2, list(range(PASSES)))
+        statistics(0)
+        norm(0)
+        statistics(1)
+        norm(1)
+        for f in range(FEAT_TILES):
+            if f + 2 < FEAT_TILES:
+                statistics(f + 2)
+            transposes_back(f)
+            if f + IN_FLIGHT < FEAT_TILES:
+                products(f + IN_FLIGHT, list(range(PASSES)))
+            store(f)
+            if f + 2 < FEAT_TILES:
+                norm(f + 2)

@@ -17,11 +17,12 @@ K_PASS = 512
 K_HALF = 256
 PASSES = K // K_PASS
 BANK = 512
+BANKS = 8
 HALVES = 2
 FEAT_TILES = FEATS // P
-ROW_TILES = ROWS // P
 BLK = 64
 JOB = 256
+JOBS = BANK // JOB
 IN_FLIGHT = 3
 EPS = 1e-5
 
@@ -32,6 +33,7 @@ def tile_attention_pb_kernel(tc, h_attn, proj_w, proj_g, proj_b, out):
     nc = tc.nc
     h_flat = h_attn.flatten_outer_dims()
     out_flat = out.flatten_outer_dims()
+    steps = [(g, half) for g in range(PASSES) for half in range(HALVES)]
 
     with tc.tile_pool(name="keep", bufs=1) as keep, tc.tile_pool(name="work", bufs=3) as work, tc.tile_pool(
         name="small", bufs=4
@@ -43,183 +45,197 @@ def tile_attention_pb_kernel(tc, h_attn, proj_w, proj_g, proj_b, out):
 
         w_raw = {}
         h_raw = {}
-        for g in range(PASSES):
-            for half in range(HALVES):
-                w_piece = keep.tile([P, BANK // P, K_PASS], BF16, name="w_raw_%d_%d" % (g, half))
+        for g, half in steps:
+            w_piece = keep.tile([P, BANK // P, K_PASS], BF16, name="w_raw_%d_%d" % (g, half))
+            nc.sync.dma_start(
+                out=w_piece[:],
+                in_=proj_w[half * BANK : (half + 1) * BANK, g * K_PASS : (g + 1) * K_PASS].rearrange(
+                    "(i p) k -> p i k", p=P
+                ),
+            )
+            w_raw[(g, half)] = w_piece
+            h_piece = keep.tile([P, BANK // BLK, K_HALF], BF16, name="h_raw_%d_%d" % (g, half))
+            for u in range(2):
+                k0 = g * K_PASS + u * K_HALF
                 nc.sync.dma_start(
-                    out=w_piece[:],
-                    in_=proj_w[half * BANK : (half + 1) * BANK, g * K_PASS : (g + 1) * K_PASS].rearrange(
-                        "(i p) k -> p i k", p=P
+                    out=h_piece[u:P:2, :, :],
+                    in_=h_flat[half * BANK : (half + 1) * BANK, k0 : k0 + K_HALF].rearrange(
+                        "(blk r) k -> r blk k", r=BLK
                     ),
                 )
-                w_raw[(g, half)] = w_piece
-                h_piece = keep.tile([P, BANK // BLK, K_HALF], BF16, name="h_raw_%d_%d" % (g, half))
-                for u in range(2):
-                    k0 = g * K_PASS + u * K_HALF
-                    nc.sync.dma_start(
-                        out=h_piece[u:P:2, :, :],
-                        in_=h_flat[half * BANK : (half + 1) * BANK, k0 : k0 + K_HALF].rearrange(
-                            "(blk r) k -> r blk k", r=BLK
-                        ),
-                    )
-                h_raw[(g, half)] = h_piece
+            h_raw[(g, half)] = h_piece
 
         ident = keep.tile([P, P], F32)
         make_identity(nc, ident[:])
+        minus_half = keep.tile([P, 1], F32)
+        nc.gpsimd.memset(minus_half[:], -0.5)
 
-        one = small.tile([P, 1], F32, tag="one")
+        one = keep.tile([P, 1], F32)
         nc.vector.memset(one[:], 1.0)
-        one_root = small.tile([P, 1], F32, tag="one_root")
-        nc.scalar.activation(out=one_root[:], in_=one[:], func=ACT.Sqrt)
+        warm = keep.tile([P, 1], F32)
+        nc.scalar.activation(out=warm[:], in_=one[:], func=ACT.Relu)
 
         gb_f32 = keep.tile([P, P], F32)
         nc.vector.tensor_copy(out=gb_f32[:], in_=gb_rows[:])
-        gb_bank = psum.tile([P, BANK], F32, tag="bank6")
+        gb_bank = psum.tile([P, BANK], F32, tag="bank%d" % (BANKS - 1))
         nc.tensor.transpose(gb_bank[:, 0:P], gb_f32[:], ident[:])
-        gb = keep.tile([P, 2 * FEAT_TILES], F32)
-        nc.vector.tensor_copy(out=gb[:], in_=gb_bank[:, 0 : 2 * FEAT_TILES])
+        gain_pm = keep.tile([P, FEAT_TILES, 2], F32)
+        nc.vector.tensor_copy(out=gain_pm[:, :, 0], in_=gb_bank[:, 0:FEAT_TILES])
+        nc.vector.tensor_scalar_mul(out=gain_pm[:, :, 1], in0=gb_bank[:, 0:FEAT_TILES], scalar1=-1.0)
+        beta = keep.tile([P, FEAT_TILES], F32)
+        nc.vector.tensor_copy(out=beta[:], in_=gb_bank[:, FEAT_TILES : 2 * FEAT_TILES])
 
-        h_codes = keep.tile([P, PASSES, ROWS], U32, align_bytes=64)
-        h_scales = keep.tile([P, PASSES, ROWS], U8, align_bytes=64)
-        w_codes = keep.tile([P, PASSES, FEATS], U32, align_bytes=64)
-        w_scales = keep.tile([P, PASSES, FEATS], U8, align_bytes=64)
+        h_codes = {}
+        h_scales = {}
+        w_codes = {}
+        w_scales = {}
+        for g, half in steps:
+            h_codes[(g, half)] = keep.tile([P, BANK], U32, align_bytes=64, name="h_codes_%d_%d" % (g, half))
+            h_scales[(g, half)] = keep.tile([P, BANK], U8, align_bytes=64, name="h_scales_%d_%d" % (g, half))
+            w_codes[(g, half)] = keep.tile([P, BANK], U32, align_bytes=64, name="w_codes_%d_%d" % (g, half))
+            w_scales[(g, half)] = keep.tile([P, BANK], U8, align_bytes=64, name="w_scales_%d_%d" % (g, half))
 
-        def quantise_w(g, half):
-            for j in range(BANK // JOB):
-                bank = psum.tile([P, 2, JOB], F32, tag="bank%d" % (6 + j))
+        h_grouped = {}
+
+        def quantise_h(s):
+            nc.vector.quantize_mx(
+                out=h_codes[steps[s]][:].bitcast(FP8X4), scales=h_scales[steps[s]][:], in_=h_grouped[s][:]
+            )
+
+        for s, step in enumerate(steps):
+            w_grouped = work.tile([P, 4 * BANK], BF16, align_bytes=64, tag="w_grouped")
+            h_grouped[s] = work.tile([P, 4 * BANK], BF16, align_bytes=64, tag="h_grouped", name="h_grouped_%d" % s)
+            for j in range(JOBS):
+                job_cols = slice(j * 4 * JOB, (j + 1) * 4 * JOB)
+                w_bank = psum.tile([P, 2, JOB], F32, tag="bank%d" % ((2 * JOBS * s + 2 * j) % BANKS))
                 for i in range(JOB // P):
                     for u in range(2):
                         nc.tensor.transpose(
-                            bank[:, u, i * P : (i + 1) * P],
-                            w_raw[(g, half)][:, j * (JOB // P) + i, u * K_HALF : (u + 1) * K_HALF].bitcast(F32),
+                            w_bank[:, u, i * P : (i + 1) * P],
+                            w_raw[step][:, j * (JOB // P) + i, u * K_HALF : (u + 1) * K_HALF].bitcast(F32),
                             ident[:],
                         )
-                w_grouped = work.tile([P, 4 * JOB], BF16, align_bytes=64, tag="w_grouped")
                 nc.scalar.copy(
-                    out=w_grouped[:].bitcast(F32).rearrange("p (c u) -> p c u", u=2),
-                    in_=bank[:].rearrange("p u c -> p c u"),
+                    out=w_grouped[:, job_cols].bitcast(F32).rearrange("p (c u) -> p c u", u=2),
+                    in_=w_bank[:].rearrange("p u c -> p c u"),
                 )
-                cols = slice(half * BANK + j * JOB, half * BANK + (j + 1) * JOB)
-                nc.vector.quantize_mx(
-                    out=w_codes[:, g, cols].bitcast(FP8X4), scales=w_scales[:, g, cols], in_=w_grouped[:]
-                )
-
-        def quantise_h(g, half):
-            h_grouped = []
-            for j in range(BANK // JOB):
-                bank = psum.tile([P, BANK], F32, tag="bank%d" % (4 + j))
+                h_bank = psum.tile([P, BANK], F32, tag="bank%d" % ((2 * JOBS * s + 2 * j + 1) % BANKS))
                 for i in range(JOB // BLK):
                     nc.tensor.transpose(
-                        bank[:, i * P : (i + 1) * P],
-                        h_raw[(g, half)][:, j * (JOB // BLK) + i, :].bitcast(F32),
+                        h_bank[:, i * P : (i + 1) * P],
+                        h_raw[step][:, j * (JOB // BLK) + i, :].bitcast(F32),
                         ident[:],
                     )
-                v = bank[:].bitcast(BF16)
+                v = h_bank[:].bitcast(BF16)
                 ramp = work.tile([P, 4 * JOB], F32, tag="ramp")
                 nc.scalar.activation(out=ramp[:], in_=v, func=ACT.Relu, bias=0.5, scale=1.0 / 6.0)
-                h_bf16 = work.tile([P, 4 * JOB], BF16, align_bytes=64, tag="h_grouped")
                 nc.vector.scalar_tensor_tensor(
-                    out=h_bf16[:], in0=ramp[:], scalar=1.0, in1=v, op0=ALU.min, op1=ALU.mult
+                    out=h_grouped[s][:, job_cols], in0=ramp[:], scalar=1.0, in1=v, op0=ALU.min, op1=ALU.mult
                 )
-                h_grouped.append(h_bf16)
-            for j in range(BANK // JOB):
-                cols = slice(half * BANK + j * JOB, half * BANK + (j + 1) * JOB)
-                nc.vector.quantize_mx(
-                    out=h_codes[:, g, cols].bitcast(FP8X4), scales=h_scales[:, g, cols], in_=h_grouped[j][:]
-                )
+                if j == 0 and s > 0:
+                    quantise_h(s - 1)
+            nc.vector.quantize_mx(out=w_codes[step][:].bitcast(FP8X4), scales=w_scales[step][:], in_=w_grouped[:])
+        quantise_h(len(steps) - 1)
 
         y = {}
 
-        def products(f, passes):
-            feats = slice(f * P, (f + 1) * P)
-            for half in range(HALVES):
-                rows = slice(half * BANK, (half + 1) * BANK)
-                if passes[0] == 0:
-                    acc = psum.tile([P, BANK], F32, tag="bank%d" % (2 * (f % IN_FLIGHT) + half))
-                    y[(f, half)] = acc
-                for g in passes:
-                    nc.tensor.matmul_mx(
-                        out=y[(f, half)][:],
-                        lhsT=w_codes[:, g, feats].bitcast(FP8X4),
-                        lhsT_scale=w_scales[:, g, feats],
-                        rhs=h_codes[:, g, rows].bitcast(FP8X4),
-                        rhs_scale=h_scales[:, g, rows],
-                        start=(g == 0),
-                        stop=(g == PASSES - 1),
-                    )
+        def products(f, half, passes):
+            feats = slice((f % (BANK // P)) * P, (f % (BANK // P) + 1) * P)
+            if passes[0] == 0:
+                y[(f, half)] = psum.tile(
+                    [P, BANK], F32, tag="bank%d" % (2 * (f % IN_FLIGHT) + half), name="y_%d_%d" % (f, half)
+                )
+            for g in passes:
+                nc.tensor.matmul_mx(
+                    out=y[(f, half)][:],
+                    lhsT=w_codes[(g, f // (BANK // P))][:, feats].bitcast(FP8X4),
+                    lhsT_scale=w_scales[(g, f // (BANK // P))][:, feats],
+                    rhs=h_codes[(g, half)][:].bitcast(FP8X4),
+                    rhs_scale=h_scales[(g, half)][:],
+                    start=(g == 0),
+                    stop=(g == PASSES - 1),
+                )
 
-        for g in range(PASSES):
-            for half in range(HALVES):
-                quantise_w(g, half)
-                quantise_h(g, half)
-                if g > 0 and half == 0:
-                    products(0, [g - 1])
-                    products(1, [g - 1])
-
-        mean_var = {}
-        std = {}
-        z = {}
+        scale_pm = {}
+        shift = {}
 
         def statistics(f):
             stats = small.tile([P, HALVES, 6], F32, tag="stats")
             for half in range(HALVES):
                 nc.vector.bn_stats(out=stats[:, half, :], in_=y[(f, half)][:])
-            mv = small.tile([P, 2], F32, tag="mean_var")
-            nc.vector.bn_aggr(out=mv[:], in_=stats[:].rearrange("p a s -> p (a s)"))
-            root = small.tile([P, 1], F32, tag="std")
-            nc.scalar.activation(out=root[:], in_=mv[:, 1:2], func=ACT.Sqrt, bias=EPS, scale=1.0)
-            mean_var[f] = mv
-            std[f] = root
+            mean_var = small.tile([P, 2], F32, tag="mean_var")
+            nc.vector.bn_aggr(out=mean_var[:], in_=stats[:].rearrange("p a s -> p (a s)"))
+            var_eps = small.tile([P, 1], F32, tag="var_eps")
+            nc.gpsimd.tensor_scalar(
+                out=var_eps[:], in0=mean_var[:, 1:2], scalar1=EPS, scalar2=1.0, op0=ALU.add, op1=ALU.mult
+            )
+            rstd = small.tile([P, 1], F32, tag="rstd")
+            nc.gpsimd.tensor_tensor(out=rstd[:], in0=var_eps[:], in1=minus_half[:], op=ALU.pow)
+            scale_pm[f] = small.tile([P, 2], F32, tag="scale_pm", name="scale_pm_%d" % f)
+            nc.gpsimd.tensor_scalar(
+                out=scale_pm[f][:], in0=gain_pm[:, f, :], scalar1=rstd[:], scalar2=1.0, op0=ALU.mult, op1=ALU.mult
+            )
+            shift[f] = small.tile([P, 1], F32, tag="shift", name="shift_%d" % f)
+            nc.gpsimd.tensor_scalar(
+                out=shift[f][:],
+                in0=mean_var[:, 0:1],
+                scalar1=scale_pm[f][:, 1:2],
+                scalar2=beta[:, f : f + 1],
+                op0=ALU.mult,
+                op1=ALU.add,
+            )
+
+        z = {}
 
         def norm(f):
-            rstd = small.tile([P, 1], F32, tag="rstd")
-            nc.vector.reciprocal(out=rstd[:], in_=std[f][:])
-            scale = small.tile([P, 1], F32, tag="scale")
-            nc.vector.tensor_mul(out=scale[:], in0=rstd[:], in1=gb[:, f : f + 1])
-            mean_scaled = small.tile([P, 1], F32, tag="mean_scaled")
-            nc.vector.tensor_mul(out=mean_scaled[:], in0=mean_var[f][:, 0:1], in1=scale[:])
-            shift = small.tile([P, 1], F32, tag="shift")
-            nc.vector.tensor_sub(out=shift[:], in0=gb[:, FEAT_TILES + f : FEAT_TILES + f + 1], in1=mean_scaled[:])
-            normed = work.tile([P, ROWS], F32, tag="z")
             for half in range(HALVES):
+                z[(f, half)] = work.tile([P, BANK], F32, tag="z%d" % half, name="z_%d_%d" % (f, half))
                 nc.scalar.activation(
-                    out=normed[:, half * BANK : (half + 1) * BANK],
+                    out=z[(f, half)][:],
                     in_=y[(f, half)][:],
                     func=ACT.Identity,
-                    bias=shift[:],
-                    scale=scale[:],
+                    bias=shift[f][:],
+                    scale=scale_pm[f][:, 0:1],
                 )
-            z[f] = normed
 
         zt = {}
 
         def transposes_back(f):
-            for j in range(2):
-                bank = psum.tile([P, ROW_TILES // 2, P], F32, tag="bank%d" % (6 + j))
-                for i in range(ROW_TILES // 2):
-                    m = j * (ROW_TILES // 2) + i
-                    nc.tensor.transpose(bank[:, i, :], z[f][:, m * P : (m + 1) * P], ident[:])
-                zt[(f, j)] = bank
+            for half in range(HALVES):
+                zt[(f, half)] = psum.tile(
+                    [P, BANK // P, P], F32, tag="bank%d" % (2 * IN_FLIGHT + half), name="zt_%d_%d" % (f, half)
+                )
+                for i in range(BANK // P):
+                    nc.tensor.transpose(zt[(f, half)][:, i, :], z[(f, half)][:, i * P : (i + 1) * P], ident[:])
 
         def store(f):
-            o = work.tile([P, ROW_TILES, P], F32, tag="o")
-            nc.vector.tensor_copy(out=o[:, 0 : ROW_TILES // 2, :], in_=zt[(f, 0)][:])
-            nc.scalar.copy(out=o[:, ROW_TILES // 2 : ROW_TILES, :], in_=zt[(f, 1)][:])
-            nc.sync.dma_start(out=out_flat[:, f * P : (f + 1) * P].rearrange("(m p) c -> p m c", p=P), in_=o[:])
+            for half in range(HALVES):
+                o = work.tile([P, BANK // P, P], F32, tag="o%d" % half)
+                if half == 0:
+                    nc.vector.tensor_copy(out=o[:], in_=zt[(f, half)][:])
+                else:
+                    nc.scalar.copy(out=o[:], in_=zt[(f, half)][:])
+                nc.sync.dma_start(
+                    out=out_flat[half * BANK : (half + 1) * BANK, f * P : (f + 1) * P].rearrange(
+                        "(m p) c -> p m c", p=P
+                    ),
+                    in_=o[:],
+                )
 
-        products(0, [PASSES - 1])
-        products(1, [PASSES - 1])
-        products(2, list(range(PASSES)))
-        statistics(0)
-        norm(0)
-        statistics(1)
-        norm(1)
+        for g in range(PASSES):
+            for f in range(IN_FLIGHT):
+                for half in range(HALVES):
+                    products(f, half, [g])
+        for f in range(IN_FLIGHT - 1):
+            statistics(f)
+            norm(f)
         for f in range(FEAT_TILES):
-            if f + 2 < FEAT_TILES:
-                statistics(f + 2)
+            if f + IN_FLIGHT - 1 < FEAT_TILES:
+                statistics(f + IN_FLIGHT - 1)
             transposes_back(f)
             if f + IN_FLIGHT < FEAT_TILES:
-                products(f + IN_FLIGHT, list(range(PASSES)))
+                for half in range(HALVES):
+                    products(f + IN_FLIGHT, half, list(range(PASSES)))
             store(f)
-            if f + 2 < FEAT_TILES:
-                norm(f + 2)
+            if f + IN_FLIGHT - 1 < FEAT_TILES:
+                norm(f + IN_FLIGHT - 1)

@@ -17,12 +17,12 @@ K_PASS = 512
 K_HALF = 256
 PASSES = K // K_PASS
 BANK = 512
-BANKS = 8
 HALVES = 2
 FEAT_TILES = FEATS // P
 BLK = 64
 JOB = 256
 JOBS = BANK // JOB
+H_BANKS = 4
 IN_FLIGHT = 3
 EPS = 1e-5
 
@@ -38,32 +38,42 @@ def tile_attention_pb_kernel(tc, h_attn, proj_w, proj_g, proj_b, out):
     with tc.tile_pool(name="keep", bufs=1) as keep, tc.tile_pool(name="work", bufs=3) as work, tc.tile_pool(
         name="small", bufs=4
     ) as small, tc.psum_pool(name="psum", bufs=1) as psum, tc.manual_schedule():
-        gb_rows = keep.tile([P, P], BF16)
-        nc.vector.memset(gb_rows[:], 0.0)
-        nc.sync.dma_start(out=gb_rows[0:FEAT_TILES, :], in_=proj_g.rearrange("(f p) -> f p", p=P))
-        nc.sync.dma_start(out=gb_rows[FEAT_TILES : 2 * FEAT_TILES, :], in_=proj_b.rearrange("(f p) -> f p", p=P))
-
-        w_raw = {}
         h_raw = {}
-        for g, half in steps:
-            w_piece = keep.tile([P, BANK // P, K_PASS], BF16, name="w_raw_%d_%d" % (g, half))
-            nc.sync.dma_start(
-                out=w_piece[:],
-                in_=proj_w[half * BANK : (half + 1) * BANK, g * K_PASS : (g + 1) * K_PASS].rearrange(
-                    "(i p) k -> p i k", p=P
-                ),
-            )
-            w_raw[(g, half)] = w_piece
-            h_piece = keep.tile([P, BANK // BLK, K_HALF], BF16, name="h_raw_%d_%d" % (g, half))
+        w_raw = {}
+
+        def load_h(g, half, j):
+            h_raw[(g, half, j)] = keep.tile([P, JOB // BLK, K_HALF], BF16, name="h_raw_%d_%d_%d" % (g, half, j))
+            row0 = half * BANK + j * JOB
             for u in range(2):
                 k0 = g * K_PASS + u * K_HALF
                 nc.sync.dma_start(
-                    out=h_piece[u:P:2, :, :],
-                    in_=h_flat[half * BANK : (half + 1) * BANK, k0 : k0 + K_HALF].rearrange(
-                        "(blk r) k -> r blk k", r=BLK
-                    ),
+                    out=h_raw[(g, half, j)][u:P:2, :, :],
+                    in_=h_flat[row0 : row0 + JOB, k0 : k0 + K_HALF].rearrange("(blk r) k -> r blk k", r=BLK),
                 )
-            h_raw[(g, half)] = h_piece
+
+        def load_w(g, half, j):
+            w_raw[(g, half, j)] = keep.tile([P, JOB // P, K_PASS], BF16, name="w_raw_%d_%d_%d" % (g, half, j))
+            feat0 = half * BANK + j * JOB
+            nc.sync.dma_start(
+                out=w_raw[(g, half, j)][:],
+                in_=proj_w[feat0 : feat0 + JOB, g * K_PASS : (g + 1) * K_PASS].rearrange("(i p) k -> p i k", p=P),
+            )
+
+        gb_rows = keep.tile([P, P], BF16)
+        nc.vector.memset(gb_rows[:], 0.0)
+
+        for s, (g, half) in enumerate(steps):
+            load_h(g, half, 0)
+            load_w(g, 0, half)
+            load_h(g, half, 1)
+            if s == 0:
+                nc.sync.dma_start(out=gb_rows[0:FEAT_TILES, :], in_=proj_g.rearrange("(f p) -> f p", p=P))
+                nc.sync.dma_start(
+                    out=gb_rows[FEAT_TILES : 2 * FEAT_TILES, :], in_=proj_b.rearrange("(f p) -> f p", p=P)
+                )
+        for g in range(PASSES):
+            for j in range(JOBS):
+                load_w(g, 1, j)
 
         ident = keep.tile([P, P], F32)
         make_identity(nc, ident[:])
@@ -75,16 +85,6 @@ def tile_attention_pb_kernel(tc, h_attn, proj_w, proj_g, proj_b, out):
         warm = keep.tile([P, 1], F32)
         nc.scalar.activation(out=warm[:], in_=one[:], func=ACT.Relu)
 
-        gb_f32 = keep.tile([P, P], F32)
-        nc.vector.tensor_copy(out=gb_f32[:], in_=gb_rows[:])
-        gb_bank = psum.tile([P, BANK], F32, tag="bank%d" % (BANKS - 1))
-        nc.tensor.transpose(gb_bank[:, 0:P], gb_f32[:], ident[:])
-        gain_pm = keep.tile([P, FEAT_TILES, 2], F32)
-        nc.vector.tensor_copy(out=gain_pm[:, :, 0], in_=gb_bank[:, 0:FEAT_TILES])
-        nc.vector.tensor_scalar_mul(out=gain_pm[:, :, 1], in0=gb_bank[:, 0:FEAT_TILES], scalar1=-1.0)
-        beta = keep.tile([P, FEAT_TILES], F32)
-        nc.vector.tensor_copy(out=beta[:], in_=gb_bank[:, FEAT_TILES : 2 * FEAT_TILES])
-
         h_codes = {}
         h_scales = {}
         w_codes = {}
@@ -95,6 +95,36 @@ def tile_attention_pb_kernel(tc, h_attn, proj_w, proj_g, proj_b, out):
             w_codes[(g, half)] = keep.tile([P, BANK], U32, align_bytes=64, name="w_codes_%d_%d" % (g, half))
             w_scales[(g, half)] = keep.tile([P, BANK], U8, align_bytes=64, name="w_scales_%d_%d" % (g, half))
 
+        def hard_swish_job(g, half, j, bank_tag, grouped):
+            h_bank = psum.tile([P, BANK], F32, tag=bank_tag)
+            for i in range(JOB // BLK):
+                nc.tensor.transpose(h_bank[:, i * P : (i + 1) * P], h_raw[(g, half, j)][:, i, :].bitcast(F32), ident[:])
+            v = h_bank[:].bitcast(BF16)
+            ramp = work.tile([P, 4 * JOB], F32, tag="ramp")
+            nc.scalar.activation(out=ramp[:], in_=v, func=ACT.Relu, bias=0.5, scale=1.0 / 6.0)
+            nc.vector.scalar_tensor_tensor(
+                out=grouped[:, j * 4 * JOB : (j + 1) * 4 * JOB],
+                in0=ramp[:],
+                scalar=1.0,
+                in1=v,
+                op0=ALU.min,
+                op1=ALU.mult,
+            )
+
+        def regroup_w_job(g, half, j, grouped):
+            w_bank = psum.tile([P, 2, JOB], F32, tag="bank%d" % (2 * IN_FLIGHT + j))
+            for i in range(JOB // P):
+                for u in range(2):
+                    nc.tensor.transpose(
+                        w_bank[:, u, i * P : (i + 1) * P],
+                        w_raw[(g, half, j)][:, i, u * K_HALF : (u + 1) * K_HALF].bitcast(F32),
+                        ident[:],
+                    )
+            nc.scalar.copy(
+                out=grouped.bitcast(F32).rearrange("p (c u) -> p c u", u=2),
+                in_=w_bank[:].rearrange("p u c -> p c u"),
+            )
+
         h_grouped = {}
 
         def quantise_h(s):
@@ -102,40 +132,38 @@ def tile_attention_pb_kernel(tc, h_attn, proj_w, proj_g, proj_b, out):
                 out=h_codes[steps[s]][:].bitcast(FP8X4), scales=h_scales[steps[s]][:], in_=h_grouped[s][:]
             )
 
-        for s, step in enumerate(steps):
-            w_grouped = work.tile([P, 4 * BANK], BF16, align_bytes=64, tag="w_grouped")
+        for s, (g, half) in enumerate(steps):
             h_grouped[s] = work.tile([P, 4 * BANK], BF16, align_bytes=64, tag="h_grouped", name="h_grouped_%d" % s)
-            for j in range(JOBS):
-                job_cols = slice(j * 4 * JOB, (j + 1) * 4 * JOB)
-                w_bank = psum.tile([P, 2, JOB], F32, tag="bank%d" % ((2 * JOBS * s + 2 * j) % BANKS))
-                for i in range(JOB // P):
-                    for u in range(2):
-                        nc.tensor.transpose(
-                            w_bank[:, u, i * P : (i + 1) * P],
-                            w_raw[step][:, j * (JOB // P) + i, u * K_HALF : (u + 1) * K_HALF].bitcast(F32),
-                            ident[:],
-                        )
-                nc.scalar.copy(
-                    out=w_grouped[:, job_cols].bitcast(F32).rearrange("p (c u) -> p c u", u=2),
-                    in_=w_bank[:].rearrange("p u c -> p c u"),
-                )
-                h_bank = psum.tile([P, BANK], F32, tag="bank%d" % ((2 * JOBS * s + 2 * j + 1) % BANKS))
-                for i in range(JOB // BLK):
-                    nc.tensor.transpose(
-                        h_bank[:, i * P : (i + 1) * P],
-                        h_raw[step][:, j * (JOB // BLK) + i, :].bitcast(F32),
-                        ident[:],
-                    )
-                v = h_bank[:].bitcast(BF16)
-                ramp = work.tile([P, 4 * JOB], F32, tag="ramp")
-                nc.scalar.activation(out=ramp[:], in_=v, func=ACT.Relu, bias=0.5, scale=1.0 / 6.0)
-                nc.vector.scalar_tensor_tensor(
-                    out=h_grouped[s][:, job_cols], in0=ramp[:], scalar=1.0, in1=v, op0=ALU.min, op1=ALU.mult
-                )
-                if j == 0 and s > 0:
-                    quantise_h(s - 1)
-            nc.vector.quantize_mx(out=w_codes[step][:].bitcast(FP8X4), scales=w_scales[step][:], in_=w_grouped[:])
+            hard_swish_job(g, half, 0, "bank%d" % (2 + (JOBS * s) % H_BANKS), h_grouped[s])
+            if s > 0:
+                quantise_h(s - 1)
+            w_grouped = work.tile([P, 4 * JOB], BF16, align_bytes=64, tag="w_grouped")
+            regroup_w_job(g, 0, half, w_grouped[:])
+            feats = slice(half * JOB, (half + 1) * JOB)
+            nc.vector.quantize_mx(
+                out=w_codes[(g, 0)][:, feats].bitcast(FP8X4), scales=w_scales[(g, 0)][:, feats], in_=w_grouped[:]
+            )
+            hard_swish_job(g, half, 1, "bank%d" % (2 + (JOBS * s + 1) % H_BANKS), h_grouped[s])
+            if s == 0:
+                gb_f32 = keep.tile([P, P], F32)
+                nc.vector.tensor_copy(out=gb_f32[:], in_=gb_rows[:])
+                gb_bank = psum.tile([P, BANK], F32, tag="bank0")
+                nc.tensor.transpose(gb_bank[:, 0:P], gb_f32[:], ident[:])
+                gain_pm = keep.tile([P, FEAT_TILES, 2], F32)
+                nc.vector.tensor_copy(out=gain_pm[:, :, 0], in_=gb_bank[:, 0:FEAT_TILES])
+                nc.vector.tensor_scalar_mul(out=gain_pm[:, :, 1], in0=gb_bank[:, 0:FEAT_TILES], scalar1=-1.0)
+                beta = keep.tile([P, FEAT_TILES], F32)
+                nc.vector.tensor_copy(out=beta[:], in_=gb_bank[:, FEAT_TILES : 2 * FEAT_TILES])
         quantise_h(len(steps) - 1)
+
+        late_w_grouped = {}
+
+        def regroup_late_w(g):
+            late_w_grouped[g] = work.tile(
+                [P, 4 * BANK], BF16, align_bytes=64, tag="late_w_grouped", name="late_w_grouped_%d" % g
+            )
+            for j in range(JOBS):
+                regroup_w_job(g, 1, j, late_w_grouped[g][:, j * 4 * JOB : (j + 1) * 4 * JOB])
 
         y = {}
 
@@ -222,20 +250,33 @@ def tile_attention_pb_kernel(tc, h_attn, proj_w, proj_g, proj_b, out):
                     in_=o[:],
                 )
 
-        for g in range(PASSES):
-            for f in range(IN_FLIGHT):
-                for half in range(HALVES):
-                    products(f, half, [g])
+        for f in range(IN_FLIGHT - 1):
+            for half in range(HALVES):
+                products(f, half, [0, 1])
+        regroup_late_w(0)
+        for f in range(IN_FLIGHT - 1):
+            products(f, 0, [2])
+        regroup_late_w(1)
+        for f in range(IN_FLIGHT - 1):
+            products(f, 1, [2])
+        regroup_late_w(2)
+        for half in range(HALVES):
+            products(IN_FLIGHT - 1, half, list(range(PASSES)))
+
         for f in range(IN_FLIGHT - 1):
             statistics(f)
             norm(f)
+        for g in range(PASSES):
+            nc.vector.quantize_mx(
+                out=w_codes[(g, 1)][:].bitcast(FP8X4), scales=w_scales[(g, 1)][:], in_=late_w_grouped[g][:]
+            )
         for f in range(FEAT_TILES):
             if f + IN_FLIGHT - 1 < FEAT_TILES:
                 statistics(f + IN_FLIGHT - 1)
-            transposes_back(f)
             if f + IN_FLIGHT < FEAT_TILES:
                 for half in range(HALVES):
                     products(f + IN_FLIGHT, half, list(range(PASSES)))
+            transposes_back(f)
             store(f)
             if f + IN_FLIGHT - 1 < FEAT_TILES:
                 norm(f + IN_FLIGHT - 1)

@@ -61,16 +61,13 @@ def tile_attention_pb_kernel(tc, h_attn, proj_w, proj_g, proj_b, out):
 
         gb_rows = keep.tile([P, P], BF16)
         nc.vector.memset(gb_rows[:], 0.0)
+        nc.scalar.dma_start(out=gb_rows[0:FEAT_TILES, :], in_=proj_g.rearrange("(f p) -> f p", p=P))
+        nc.scalar.dma_start(out=gb_rows[FEAT_TILES : 2 * FEAT_TILES, :], in_=proj_b.rearrange("(f p) -> f p", p=P))
 
-        for s, (g, half) in enumerate(steps):
+        for g, half in steps:
             load_h(g, half, 0)
             load_w(g, 0, half)
             load_h(g, half, 1)
-            if s == 0:
-                nc.sync.dma_start(out=gb_rows[0:FEAT_TILES, :], in_=proj_g.rearrange("(f p) -> f p", p=P))
-                nc.sync.dma_start(
-                    out=gb_rows[FEAT_TILES : 2 * FEAT_TILES, :], in_=proj_b.rearrange("(f p) -> f p", p=P)
-                )
         for g in range(PASSES):
             for j in range(JOBS):
                 load_w(g, 1, j)
@@ -84,6 +81,9 @@ def tile_attention_pb_kernel(tc, h_attn, proj_w, proj_g, proj_b, out):
         nc.vector.memset(one[:], 1.0)
         warm = keep.tile([P, 1], F32)
         nc.scalar.activation(out=warm[:], in_=one[:], func=ACT.Relu)
+
+        gb_f32 = keep.tile([P, P], F32)
+        nc.vector.tensor_copy(out=gb_f32[:], in_=gb_rows[:])
 
         h_codes = {}
         h_scales = {}
@@ -145,15 +145,13 @@ def tile_attention_pb_kernel(tc, h_attn, proj_w, proj_g, proj_b, out):
             )
             hard_swish_job(g, half, 1, "bank%d" % (2 + (JOBS * s + 1) % H_BANKS), h_grouped[s])
             if s == 0:
-                gb_f32 = keep.tile([P, P], F32)
-                nc.vector.tensor_copy(out=gb_f32[:], in_=gb_rows[:])
                 gb_bank = psum.tile([P, BANK], F32, tag="bank0")
                 nc.tensor.transpose(gb_bank[:, 0:P], gb_f32[:], ident[:])
                 gain_pm = keep.tile([P, FEAT_TILES, 2], F32)
-                nc.vector.tensor_copy(out=gain_pm[:, :, 0], in_=gb_bank[:, 0:FEAT_TILES])
-                nc.vector.tensor_scalar_mul(out=gain_pm[:, :, 1], in0=gb_bank[:, 0:FEAT_TILES], scalar1=-1.0)
+                nc.scalar.copy(out=gain_pm[:, :, 0], in_=gb_bank[:, 0:FEAT_TILES])
+                nc.scalar.mul(out=gain_pm[:, :, 1], in_=gb_bank[:, 0:FEAT_TILES], mul=-1.0)
                 beta = keep.tile([P, FEAT_TILES], F32)
-                nc.vector.tensor_copy(out=beta[:], in_=gb_bank[:, FEAT_TILES : 2 * FEAT_TILES])
+                nc.scalar.copy(out=beta[:], in_=gb_bank[:, FEAT_TILES : 2 * FEAT_TILES])
         quantise_h(len(steps) - 1)
 
         late_w_grouped = {}

@@ -271,10 +271,10 @@ def tile_attention_pb_kernel(tc, h_attn, proj_w, proj_g, proj_b, out):
         for f in range(FEAT_TILES):
             if f + IN_FLIGHT - 1 < FEAT_TILES:
                 statistics(f + IN_FLIGHT - 1)
+            transposes_back(f)
             if f + IN_FLIGHT < FEAT_TILES:
                 for half in range(HALVES):
                     products(f + IN_FLIGHT, half, list(range(PASSES)))
-            transposes_back(f)
             store(f)
             if f + IN_FLIGHT - 1 < FEAT_TILES:
                 norm(f + IN_FLIGHT - 1)

import concourse.mybir as mybir
from concourse.masks import make_identity

F32 = mybir.dt.float32
BF16 = mybir.dt.bfloat16
U32 = mybir.dt.uint32
U8 = mybir.dt.uint8
FP8X4 = mybir.dt.float8_e4m3fn_x4
ACT = mybir.ActivationFunctionType
ALU = mybir.AluOpType

P = 128
ROWS = 1024
FEATS = 1024
K = 1536
K_PASS = 512
K_HALF = 256
PASSES = K // K_PASS
BANK = 512
HALVES = 2
FEAT_TILES = FEATS // P
BLK = 64
JOB = 256
JOBS = BANK // JOB
H_BANKS = 4
IN_FLIGHT = 3
EPS = 1e-5

FLOPS = 2 * ROWS * FEATS * K


def tile_attention_pb_kernel(tc, h_attn, proj_w, proj_g, proj_b, out):
    nc = tc.nc
    h_flat = h_attn.flatten_outer_dims()
    out_flat = out.flatten_outer_dims()
    steps = [(g, half) for g in range(PASSES) for half in range(HALVES)]

    with tc.tile_pool(name="keep", bufs=1) as keep, tc.tile_pool(name="work", bufs=3) as work, tc.tile_pool(
        name="small", bufs=4
    ) as small, tc.psum_pool(name="psum", bufs=1) as psum, tc.manual_schedule():
        h_raw = {}
        w_raw = {}

        def load_h(g, half, j):
            h_raw[(g, half, j)] = keep.tile([P, JOB // BLK, K_HALF], BF16, name="h_raw_%d_%d_%d" % (g, half, j))
            row0 = half * BANK + j * JOB
            for u in range(2):
                k0 = g * K_PASS + u * K_HALF
                nc.sync.dma_start(
                    out=h_raw[(g, half, j)][u:P:2, :, :],
                    in_=h_flat[row0 : row0 + JOB, k0 : k0 + K_HALF].rearrange("(blk r) k -> r blk k", r=BLK),
                )

        def load_w(g, half, j):
            w_raw[(g, half, j)] = keep.tile([P, JOB // P, K_PASS], BF16, name="w_raw_%d_%d_%d" % (g, half, j))
            feat0 = half * BANK + j * JOB
            nc.sync.dma_start(
                out=w_raw[(g, half, j)][:],
                in_=proj_w[feat0 : feat0 + JOB, g * K_PASS : (g + 1) * K_PASS].rearrange("(i p) k -> p i k", p=P),
            )

        gb_rows = keep.tile([P, P], BF16)
        nc.vector.memset(gb_rows[:], 0.0)
        nc.scalar.dma_start(out=gb_rows[0:FEAT_TILES, :], in_=proj_g.rearrange("(f p) -> f p", p=P))
        nc.scalar.dma_start(out=gb_rows[FEAT_TILES : 2 * FEAT_TILES, :], in_=proj_b.rearrange("(f p) -> f p", p=P))

        for g, half in steps:
            load_h(g, half, 0)
            load_w(g, 0, half)
            load_h(g, half, 1)
        for g in range(PASSES):
            for j in range(JOBS):
                load_w(g, 1, j)

        ident = keep.tile([P, P], F32)
        make_identity(nc, ident[:])
        minus_half = keep.tile([P, 1], F32)
        nc.gpsimd.memset(minus_half[:], -0.5)

        one = keep.tile([P, 1], F32)
        nc.vector.memset(one[:], 1.0)
        warm = keep.tile([P, 1], F32)
        nc.scalar.activation(out=warm[:], in_=one[:], func=ACT.Relu)

        gb_f32 = keep.tile([P, P], F32)
        nc.vector.tensor_copy(out=gb_f32[:], in_=gb_rows[:])

        h_codes = {}
        h_scales = {}
        w_codes = {}
        w_scales = {}
        for g, half in steps:
            h_codes[(g, half)] = keep.tile([P, BANK], U32, align_bytes=64, name="h_codes_%d_%d" % (g, half))
            h_scales[(g, half)] = keep.tile([P, BANK], U8, align_bytes=64, name="h_scales_%d_%d" % (g, half))
            w_codes[(g, half)] = keep.tile([P, BANK], U32, align_bytes=64, name="w_codes_%d_%d" % (g, half))
            w_scales[(g, half)] = keep.tile([P, BANK], U8, align_bytes=64, name="w_scales_%d_%d" % (g, half))

        def hard_swish_job(g, half, j, bank_tag, grouped):
            h_bank = psum.tile([P, BANK], F32, tag=bank_tag)
            for i in range(JOB // BLK):
                nc.tensor.transpose(h_bank[:, i * P : (i + 1) * P], h_raw[(g, half, j)][:, i, :].bitcast(F32), ident[:])
            v = h_bank[:].bitcast(BF16)
            ramp = work.tile([P, 4 * JOB], F32, tag="ramp")
            nc.scalar.activation(out=ramp[:], in_=v, func=ACT.Relu, bias=0.5, scale=1.0 / 6.0)
            nc.vector.scalar_tensor_tensor(
                out=grouped[:, j * 4 * JOB : (j + 1) * 4 * JOB],
                in0=ramp[:],
                scalar=1.0,
                in1=v,
                op0=ALU.min,
                op1=ALU.mult,
            )

        def regroup_w_job(g, half, j, grouped):
            w_bank = psum.tile([P, 2, JOB], F32, tag="bank%d" % (2 * IN_FLIGHT + j))
            for i in range(JOB // P):
                for u in range(2):
                    nc.tensor.transpose(
                        w_bank[:, u, i * P : (i + 1) * P],
                        w_raw[(g, half, j)][:, i, u * K_HALF : (u + 1) * K_HALF].bitcast(F32),
                        ident[:],
                    )
            nc.scalar.copy(
                out=grouped.bitcast(F32).rearrange("p (c u) -> p c u", u=2),
                in_=w_bank[:].rearrange("p u c -> p c u"),
            )

        h_grouped = {}

        def quantise_h(s):
            nc.vector.quantize_mx(
                out=h_codes[steps[s]][:].bitcast(FP8X4), scales=h_scales[steps[s]][:], in_=h_grouped[s][:]
            )

        for s, (g, half) in enumerate(steps):
            h_grouped[s] = work.tile([P, 4 * BANK], BF16, align_bytes=64, tag="h_grouped", name="h_grouped_%d" % s)
            hard_swish_job(g, half, 0, "bank%d" % (2 + (JOBS * s) % H_BANKS), h_grouped[s])
            if s > 0:
                quantise_h(s - 1)
            w_grouped = work.tile([P, 4 * JOB], BF16, align_bytes=64, tag="w_grouped")
            regroup_w_job(g, 0, half, w_grouped[:])
            feats = slice(half * JOB, (half + 1) * JOB)
            nc.vector.quantize_mx(
                out=w_codes[(g, 0)][:, feats].bitcast(FP8X4), scales=w_scales[(g, 0)][:, feats], in_=w_grouped[:]
            )
            hard_swish_job(g, half, 1, "bank%d" % (2 + (JOBS * s + 1) % H_BANKS), h_grouped[s])
            if s == 0:
                gb_bank = psum.tile([P, BANK], F32, tag="bank0")
                nc.tensor.transpose(gb_bank[:, 0:P], gb_f32[:], ident[:])
                gain_pm = keep.tile([P, FEAT_TILES, 2], F32)
                nc.scalar.copy(out=gain_pm[:, :, 0], in_=gb_bank[:, 0:FEAT_TILES])
                nc.scalar.mul(out=gain_pm[:, :, 1], in_=gb_bank[:, 0:FEAT_TILES], mul=-1.0)
                beta = keep.tile([P, FEAT_TILES], F32)
                nc.scalar.copy(out=beta[:], in_=gb_bank[:, FEAT_TILES : 2 * FEAT_TILES])
        quantise_h(len(steps) - 1)

        late_w_grouped = {}

        def regroup_late_w(g):
            late_w_grouped[g] = work.tile(
                [P, 4 * BANK], BF16, align_bytes=64, tag="late_w_grouped", name="late_w_grouped_%d" % g
            )
            for j in range(JOBS):
                regroup_w_job(g, 1, j, late_w_grouped[g][:, j * 4 * JOB : (j + 1) * 4 * JOB])

        y = {}

        def products(f, half, passes):
            feats = slice((f % (BANK // P)) * P, (f % (BANK // P) + 1) * P)
            if passes[0] == 0:
                y[(f, half)] = psum.tile(
                    [P, BANK], F32, tag="bank%d" % (2 * (f % IN_FLIGHT) + half), name="y_%d_%d" % (f, half)
                )
            for g in passes:
                nc.tensor.matmul_mx(
                    out=y[(f, half)][:],
                    lhsT=w_codes[(g, f // (BANK // P))][:, feats].bitcast(FP8X4),
                    lhsT_scale=w_scales[(g, f // (BANK // P))][:, feats],
                    rhs=h_codes[(g, half)][:].bitcast(FP8X4),
                    rhs_scale=h_scales[(g, half)][:],
                    start=(g == 0),
                    stop=(g == PASSES - 1),
                )

        scale_pm = {}
        shift = {}

        def statistics(f):
            stats = small.tile([P, HALVES, 6], F32, tag="stats")
            for half in range(HALVES):
                nc.vector.bn_stats(out=stats[:, half, :], in_=y[(f, half)][:])
            mean_var = small.tile([P, 2], F32, tag="mean_var")
            nc.vector.bn_aggr(out=mean_var[:], in_=stats[:].rearrange("p a s -> p (a s)"))
            var_eps = small.tile([P, 1], F32, tag="var_eps")
            nc.gpsimd.tensor_scalar(
                out=var_eps[:], in0=mean_var[:, 1:2], scalar1=EPS, scalar2=1.0, op0=ALU.add, op1=ALU.mult
            )
            rstd = small.tile([P, 1], F32, tag="rstd")
            nc.gpsimd.tensor_tensor(out=rstd[:], in0=var_eps[:], in1=minus_half[:], op=ALU.pow)
            scale_pm[f] = small.tile([P, 2], F32, tag="scale_pm", name="scale_pm_%d" % f)
            nc.gpsimd.tensor_scalar(
                out=scale_pm[f][:], in0=gain_pm[:, f, :], scalar1=rstd[:], scalar2=1.0, op0=ALU.mult, op1=ALU.mult
            )
            shift[f] = small.tile([P, 1], F32, tag="shift", name="shift_%d" % f)
            nc.gpsimd.tensor_scalar(
                out=shift[f][:],
                in0=mean_var[:, 0:1],
                scalar1=scale_pm[f][:, 1:2],
                scalar2=beta[:, f : f + 1],
                op0=ALU.mult,
                op1=ALU.add,
            )

        z = {}

        def norm(f):
            for half in range(HALVES):
                z[(f, half)] = work.tile([P, BANK], F32, tag="z%d" % half, name="z_%d_%d" % (f, half))
                nc.scalar.activation(
                    out=z[(f, half)][:],
                    in_=y[(f, half)][:],
                    func=ACT.Identity,
                    bias=shift[f][:],
                    scale=scale_pm[f][:, 0:1],
                )

        zt = {}

        def transposes_back(f):
            for half in range(HALVES):
                zt[(f, half)] = psum.tile(
                    [P, BANK // P, P], F32, tag="bank%d" % (2 * IN_FLIGHT + half), name="zt_%d_%d" % (f, half)
                )
                for i in range(BANK // P):
                    nc.tensor.transpose(zt[(f, half)][:, i, :], z[(f, half)][:, i * P : (i + 1) * P], ident[:])

        def store(f):
            for half in range(HALVES):
                o = work.tile([P, BANK // P, P], F32, tag="o%d" % half)
                if half == 0:
                    nc.vector.tensor_copy(out=o[:], in_=zt[(f, half)][:])
                else:
                    nc.scalar.copy(out=o[:], in_=zt[(f, half)][:])
                nc.sync.dma_start(
                    out=out_flat[half * BANK : (half + 1) * BANK, f * P : (f + 1) * P].rearrange(
                        "(m p) c -> p m c", p=P
                    ),
                    in_=o[:],
                )

        for f in range(IN_FLIGHT - 1):
            for half in range(HALVES):
                products(f, half, [0, 1])
        regroup_late_w(0)
        for f in range(IN_FLIGHT - 1):
            products(f, 0, [2])
        regroup_late_w(1)
        for f in range(IN_FLIGHT - 1):
            products(f, 1, [2])
        regroup_late_w(2)
        for half in range(HALVES):
            products(IN_FLIGHT - 1, half, list(range(PASSES)))

        for f in range(IN_FLIGHT - 1):
            statistics(f)
            norm(f)
        for g in range(PASSES):
            nc.vector.quantize_mx(
                out=w_codes[(g, 1)][:].bitcast(FP8X4), scales=w_scales[(g, 1)][:], in_=late_w_grouped[g][:]
            )
        for f in range(FEAT_TILES):
            if f + IN_FLIGHT - 1 < FEAT_TILES:
                statistics(f + IN_FLIGHT - 1)
            transposes_back(f)
            if f + IN_FLIGHT < FEAT_TILES:
                for half in range(HALVES):
                    products(f + IN_FLIGHT, half, list(range(PASSES)))
            store(f)
            if f + IN_FLIGHT - 1 < FEAT_TILES:
                norm(f + IN_FLIGHT - 1)
